import numpy as np
import ml_dtypes

BF16 = ml_dtypes.bfloat16


def bf(x):
    return np.asarray(x, np.float32).astype(BF16)


def f32(x):
    return np.asarray(x, np.float32)


def f64(x):
    return np.asarray(x).astype(np.float64)


def striped(idx):
    return np.tile(idx.reshape(-1, 16).T, (8, 1))


C, S, M, T, K, H, N = 128, 1024, 256, 3, 6, 512, 3072
EPS = 1e-5


def setup_inputs():
    sc = 1.0 / np.sqrt(T * C)
    return {"x": bf(np.random.standard_normal((C, S))), "w_self": bf(sc * np.random.standard_normal((C, M))), "w_left": bf(sc * np.random.standard_normal((C, M))), "w_right": bf(sc * np.random.standard_normal((C, M))), "b": f32(0.1 * np.random.standard_normal((M, 1))), "offs": striped(np.concatenate([np.random.permutation(S)[:H] for _ in range(K)]))}


def reference(x, w_self, w_left, w_right, b, offs):
    idx = offs[:16].T.reshape(-1)
    tap = idx.reshape(T, S)
    xs = f64(x)
    y = f64(w_self).T @ xs[:, tap[0]] + f64(w_left).T @ xs[:, tap[1]] + f64(w_right).T @ xs[:, tap[2]] + f64(b)
    mu = y.mean()
    sd = np.sqrt(np.square(y - mu).sum() / (M * S - 1))
    return np.maximum((y - mu) / (sd + EPS), 0.0)

@@ -1,0 +1,130 @@
+import concourse.mybir as mybir
+
+BF16, F32, U16 = mybir.dt.bfloat16, mybir.dt.float32, mybir.dt.uint16
+ALU = mybir.AluOpType
+ACT = mybir.ActivationFunctionType
+
+P = 128
+NODES = 1024
+FEATURES = 256
+TAPS = 3
+BLOCKS = FEATURES // P
+BANK = 512
+EPS = 1e-5
+
+PIECES = (
+    ((0, 512), (512, 512)),
+    ((0, 512), (512, 384), (896, 128)),
+)
+N_PIECES = sum(len(cut) for cut in PIECES)
+
+FLOPS = 2 * TAPS * P * FEATURES * NODES
+
+
+def tile_net_latency_kernel(tc, x, w_self, w_left, w_right, b, offs, out):
+    nc = tc.nc
+    with (
+        tc.tile_pool(name="held", bufs=1) as held,
+        tc.psum_pool(name="psum", bufs=1) as psum,
+    ):
+        offsets = held.tile([P, TAPS * NODES // 16], U16, name="offsets")
+        nc.sync.dma_start(offsets[:], offs)
+        table = held.tile([P, NODES], BF16, name="table")
+        nc.scalar.dma_start(table[:], x)
+        weights = []
+        for tap, w in enumerate((w_self, w_left, w_right)):
+            w_tile = held.tile([P, FEATURES], BF16, name=f"w{tap}")
+            nc.sync.dma_start(w_tile[:], w)
+            weights.append(w_tile)
+        bias = held.tile([P, BLOCKS], F32, name="bias")
+        with nc.allow_non_contiguous_dma(reason="256 floats, one to a partition and block"):
+            nc.sync.dma_start(bias[:], b.rearrange("(k p) o -> p (k o)", p=P))
+
+        last_bias = bias[:, BLOCKS - 1 : BLOCKS]
+        rel_bias = held.tile([P, BLOCKS], F32, name="rel_bias")
+        nc.vector.tensor_scalar(rel_bias[:], bias[:], last_bias, None, ALU.subtract)
+
+        averager = held.tile([P, P], F32, name="averager")
+        nc.vector.memset(averager[:], 1.0 / P)
+        centring = held.tile([P, P], F32, name="centring")
+        nc.gpsimd.memset(centring[:], -1.0 / P)
+        nc.gpsimd.affine_select(
+            out=centring[:],
+            in_=centring[:],
+            compare_op=ALU.not_equal,
+            fill=1.0 - 1.0 / P,
+            base=0,
+            pattern=[[-1, P]],
+            channel_multiplier=1,
+        )
+
+        n = FEATURES * NODES
+        bessel = n / (n - 1.0)
+        spread = held.tile([P, 2], F32, name="spread")
+        nc.vector.memset(spread[:, 1:2], EPS * EPS / bessel)
+
+        stats = held.tile([P, N_PIECES * 6], F32, name="stats")
+        y = []
+        for block, cut in enumerate(PIECES):
+            block_start = len(y) * 6
+            banks = [psum.tile([P, nodes], F32, name=f"y{len(y) + i}") for i, (first, nodes) in enumerate(cut)]
+            if block < BLOCKS - 1:
+                order = [(tap, i) for tap in range(TAPS) for i in range(len(cut))]
+            else:
+                order = [(tap, i) for i in range(len(cut)) for tap in range(TAPS)]
+            for tap, i in order:
+                first, nodes = cut[i]
+                column = (tap * NODES + first) // 16
+                nc.tensor.matmul(
+                    banks[i][:],
+                    weights[tap][:, block * P : (block + 1) * P],
+                    table[:].indirect(offsets[:, column : column + nodes // 16]),
+                    start=(tap == 0),
+                    stop=(tap == TAPS - 1),
+                )
+                if tap == TAPS - 1:
+                    nc.vector.bn_stats(stats[:, len(y) * 6 : (len(y) + 1) * 6], banks[i][:])
+                    y.append((block, first, nodes, banks[i]))
+            if block < BLOCKS - 1:
+                triples = stats[:, block_start : len(y) * 6]
+                means = triples.rearrange("p (t c) -> p t c", c=3)[:, :, 1:2]
+                nc.vector.tensor_scalar(means, means, rel_bias[:, block : block + 1], None, ALU.add)
+
+        row = held.tile([P, 2], F32, name="row")
+        nc.vector.bn_aggr(row[:], stats[:])
+        row_mean, row_var = row[:, 0:1], row[:, 1:2]
+        off_mean = psum.tile([P, 1], F32, name="off_mean")
+        nc.tensor.matmul(off_mean[:], centring[:], last_bias, start=True, stop=False)
+        nc.tensor.matmul(off_mean[:], centring[:], row_mean, start=False, stop=True)
+        nc.vector.scalar_tensor_tensor(
+            spread[:, 0:1], off_mean[:], off_mean[:], row_var, ALU.mult, ALU.add
+        )
+        var_psum = psum.tile([P, 2], F32, name="var_psum")
+        nc.tensor.matmul(var_psum[:], averager[:], spread[:], start=True, stop=True)
+        centre = held.tile([P, BLOCKS], F32, name="centre")
+        nc.vector.tensor_scalar(centre[:], rel_bias[:], row_mean, off_mean[:], ALU.subtract, ALU.add)
+        short = [piece for piece in y if piece[2] < BANK]
+        whole = [piece for piece in y if piece[2] == BANK]
+        centred = []
+        for block, first, nodes, y_piece in short:
+            y_less_mu = held.tile([P, nodes], F32, name=f"normed{block}_{first}")
+            nc.vector.tensor_scalar(y_less_mu[:], y_piece[:], centre[:, block : block + 1], None, ALU.add)
+            centred.append(y_less_mu)
+
+        roots = held.tile([P, 2], F32, name="roots")
+        sd_eps = held.tile([P, 1], F32, name="sd_eps")
+        nc.scalar.activation(roots[:], var_psum[:], ACT.Sqrt, scale=bessel, accum_out=sd_eps[:])
+        gain = held.tile([P, 1], F32, name="gain")
+        nc.vector.reciprocal(gain[:], sd_eps[:])
+        shift = held.tile([P, BLOCKS], F32, name="shift")
+        nc.vector.tensor_scalar(shift[:], centre[:], gain[:], None, ALU.mult)
+
+        for (block, first, nodes, y_piece), y_less_mu in zip(short, centred):
+            nc.vector.tensor_scalar(y_less_mu[:], y_less_mu[:], gain[:], 0.0, ALU.mult, ALU.max)
+            nc.sync.dma_start(out[block * P : (block + 1) * P, first : first + nodes], y_less_mu[:])
+        for block, first, nodes, y_piece in whole:
+            normed = held.tile([P, nodes], F32, name=f"normed{block}_{first}")
+            nc.scalar.activation(
+                normed[:], y_piece[:], ACT.Relu, bias=shift[:, block : block + 1], scale=gain[:]
+            )
+            nc.sync.dma_start(out[block * P : (block + 1) * P, first : first + nodes], normed[:])

@@ -117,14 +117,22 @@ def tile_net_latency_kernel(tc, x, w_self, w_left, w_right, b, offs, out):
         gain = held.tile([P, 1], F32, name="gain")
         nc.vector.reciprocal(gain[:], sd_eps[:])
         shift = held.tile([P, BLOCKS], F32, name="shift")
-        nc.vector.tensor_scalar(shift[:], centre[:], gain[:], None, ALU.mult)
+        nc.scalar.activation(shift[:], centre[:], ACT.Identity, scale=gain[:])
 
-        for (block, first, nodes, y_piece), y_less_mu in zip(short, centred):
+        for (block, first, nodes, y_piece), y_less_mu in reversed(list(zip(short, centred))):
             nc.vector.tensor_scalar(y_less_mu[:], y_less_mu[:], gain[:], 0.0, ALU.mult, ALU.max)
             nc.sync.dma_start(out[block * P : (block + 1) * P, first : first + nodes], y_less_mu[:])
+        half = BANK // 2
         for block, first, nodes, y_piece in whole:
-            normed = held.tile([P, nodes], F32, name=f"normed{block}_{first}")
-            nc.scalar.activation(
-                normed[:], y_piece[:], ACT.Relu, bias=shift[:, block : block + 1], scale=gain[:]
-            )
-            nc.sync.dma_start(out[block * P : (block + 1) * P, first : first + nodes], normed[:])
+            for start in range(0, BANK, half):
+                normed = held.tile([P, half], F32, name=f"normed{block}_{first + start}")
+                nc.scalar.activation(
+                    normed[:],
+                    y_piece[:, start : start + half],
+                    ACT.Relu,
+                    bias=shift[:, block : block + 1],
+                    scale=gain[:],
+                )
+                nc.sync.dma_start(
+                    out[block * P : (block + 1) * P, first + start : first + start + half], normed[:]
+                )

@@ -122,17 +122,9 @@ def tile_net_latency_kernel(tc, x, w_self, w_left, w_right, b, offs, out):
         for (block, first, nodes, y_piece), y_less_mu in reversed(list(zip(short, centred))):
             nc.vector.tensor_scalar(y_less_mu[:], y_less_mu[:], gain[:], 0.0, ALU.mult, ALU.max)
             nc.sync.dma_start(out[block * P : (block + 1) * P, first : first + nodes], y_less_mu[:])
-        half = BANK // 2
         for block, first, nodes, y_piece in whole:
-            for start in range(0, BANK, half):
-                normed = held.tile([P, half], F32, name=f"normed{block}_{first + start}")
-                nc.scalar.activation(
-                    normed[:],
-                    y_piece[:, start : start + half],
-                    ACT.Relu,
-                    bias=shift[:, block : block + 1],
-                    scale=gain[:],
-                )
-                nc.sync.dma_start(
-                    out[block * P : (block + 1) * P, first + start : first + start + half], normed[:]
-                )
+            normed = held.tile([P, nodes], F32, name=f"normed{block}_{first}")
+            nc.scalar.activation(
+                normed[:], y_piece[:], ACT.Relu, bias=shift[:, block : block + 1], scale=gain[:]
+            )
+            nc.sync.dma_start(out[block * P : (block + 1) * P, first : first + nodes], normed[:])

@@ -11,6 +11,7 @@ TAPS = 3
 BLOCKS = FEATURES // P
 BANK = 512
 EPS = 1e-5
+NEVER_NEGATIVE = (1e-3 * EPS) ** 2
 
 PIECES = (
     ((0, 512), (512, 512)),
@@ -40,28 +41,18 @@ def tile_net_latency_kernel(tc, x, w_self, w_left, w_right, b, offs, out):
         with nc.allow_non_contiguous_dma(reason="256 floats, one to a partition and block"):
             nc.sync.dma_start(bias[:], b.rearrange("(k p) o -> p (k o)", p=P))
 
-        last_bias = bias[:, BLOCKS - 1 : BLOCKS]
-        rel_bias = held.tile([P, BLOCKS], F32, name="rel_bias")
-        nc.vector.tensor_scalar(rel_bias[:], bias[:], last_bias, None, ALU.subtract)
-
         averager = held.tile([P, P], F32, name="averager")
         nc.vector.memset(averager[:], 1.0 / P)
-        centring = held.tile([P, P], F32, name="centring")
-        nc.gpsimd.memset(centring[:], -1.0 / P)
-        nc.gpsimd.affine_select(
-            out=centring[:],
-            in_=centring[:],
-            compare_op=ALU.not_equal,
-            fill=1.0 - 1.0 / P,
-            base=0,
-            pattern=[[-1, P]],
-            channel_multiplier=1,
-        )
-
         n = FEATURES * NODES
         bessel = n / (n - 1.0)
         spread = held.tile([P, 2], F32, name="spread")
-        nc.vector.memset(spread[:, 1:2], EPS * EPS / bessel)
+        nc.vector.memset(spread[:, 1:2], -EPS * EPS / bessel)
+        roots = held.tile([P, 2], F32, name="roots")
+        nc.scalar.activation(roots[:, 1:2], spread[:, 1:2], ACT.Sqrt, bias=NEVER_NEGATIVE, scale=-bessel)
+
+        last_bias = bias[:, BLOCKS - 1 : BLOCKS]
+        rel_bias = held.tile([P, BLOCKS], F32, name="rel_bias")
+        nc.vector.tensor_scalar(rel_bias[:], bias[:], last_bias, None, ALU.subtract)
 
         stats = held.tile([P, N_PIECES * 6], F32, name="stats")
         y = []
@@ -84,6 +75,9 @@ def tile_net_latency_kernel(tc, x, w_self, w_left, w_right, b, offs, out):
                 )
                 if tap == TAPS - 1:
                     nc.vector.bn_stats(stats[:, len(y) * 6 : (len(y) + 1) * 6], banks[i][:])
+                    if not y:
+                        sample = held.tile([P, 1], F32, name="sample")
+                        nc.vector.tensor_scalar(sample[:], stats[:, 1:2], bias[:, block : block + 1], None, ALU.add)
                     y.append((block, first, nodes, banks[i]))
             if block < BLOCKS - 1:
                 triples = stats[:, block_start : len(y) * 6]
@@ -92,36 +86,45 @@ def tile_net_latency_kernel(tc, x, w_self, w_left, w_right, b, offs, out):
 
         row = held.tile([P, 2], F32, name="row")
         nc.vector.bn_aggr(row[:], stats[:])
-        row_mean, row_var = row[:, 0:1], row[:, 1:2]
-        off_mean = psum.tile([P, 1], F32, name="off_mean")
-        nc.tensor.matmul(off_mean[:], centring[:], last_bias, start=True, stop=False)
-        nc.tensor.matmul(off_mean[:], centring[:], row_mean, start=False, stop=True)
-        nc.vector.scalar_tensor_tensor(
-            spread[:, 0:1], off_mean[:], off_mean[:], row_var, ALU.mult, ALU.add
+        pivot = psum.tile([P, 1], F32, name="pivot")
+        nc.tensor.matmul(pivot[:], averager[:], sample[:], start=True, stop=True)
+        terms = held.tile([P, BLOCKS + 1], F32, name="terms")
+        pivoted_bias, last_terms = terms[:, 0:BLOCKS], terms[:, BLOCKS - 1 : BLOCKS + 1]
+        nc.vector.tensor_scalar(pivoted_bias, bias[:], pivot[:], None, ALU.subtract)
+        nc.scalar.activation(
+            terms[:, BLOCKS : BLOCKS + 1], row[:, 0:1], ACT.Square, bias=terms[:, BLOCKS - 1 : BLOCKS]
         )
-        var_psum = psum.tile([P, 2], F32, name="var_psum")
-        nc.tensor.matmul(var_psum[:], averager[:], spread[:], start=True, stop=True)
-        centre = held.tile([P, BLOCKS], F32, name="centre")
-        nc.vector.tensor_scalar(centre[:], rel_bias[:], row_mean, off_mean[:], ALU.subtract, ALU.add)
+        moments = psum.tile([P, 2], F32, name="moments")
+        nc.tensor.matmul(moments[:], averager[:], row[:], start=True, stop=False)
+        nc.tensor.matmul(moments[:], averager[:], last_terms, start=False, stop=True)
+        m, mean_square = moments[:, 0:1], moments[:, 1:2]
+
         short = [piece for piece in y if piece[2] < BANK]
         whole = [piece for piece in y if piece[2] == BANK]
         centred = []
-        for block, first, nodes, y_piece in short:
-            y_less_mu = held.tile([P, nodes], F32, name=f"normed{block}_{first}")
-            nc.vector.tensor_scalar(y_less_mu[:], y_piece[:], centre[:, block : block + 1], None, ALU.add)
-            centred.append(y_less_mu)
+        for block, first, nodes, y_piece in reversed(short):
+            z = held.tile([P, nodes], F32, name=f"z{block}_{first}")
+            nc.vector.tensor_scalar(z[:], y_piece[:], terms[:, block : block + 1], None, ALU.add)
+            centred.append(z)
 
-        roots = held.tile([P, 2], F32, name="roots")
+        nc.vector.tensor_scalar(spread[:, 0:1], m, m, mean_square, ALU.mult, ALU.subtract)
+        centre = held.tile([P, BLOCKS], F32, name="centre")
+        nc.vector.tensor_scalar(centre[:], pivoted_bias, m, None, ALU.subtract)
+        for z in centred:
+            nc.vector.tensor_scalar(z[:], z[:], m, None, ALU.subtract)
+
         sd_eps = held.tile([P, 1], F32, name="sd_eps")
-        nc.scalar.activation(roots[:], var_psum[:], ACT.Sqrt, scale=bessel, accum_out=sd_eps[:])
+        nc.scalar.activation(
+            roots[:], spread[:], ACT.Sqrt, bias=NEVER_NEGATIVE, scale=-bessel, accum_out=sd_eps[:]
+        )
         gain = held.tile([P, 1], F32, name="gain")
         nc.vector.reciprocal(gain[:], sd_eps[:])
         shift = held.tile([P, BLOCKS], F32, name="shift")
         nc.scalar.activation(shift[:], centre[:], ACT.Identity, scale=gain[:])
 
-        for (block, first, nodes, y_piece), y_less_mu in reversed(list(zip(short, centred))):
-            nc.vector.tensor_scalar(y_less_mu[:], y_less_mu[:], gain[:], 0.0, ALU.mult, ALU.max)
-            nc.sync.dma_start(out[block * P : (block + 1) * P, first : first + nodes], y_less_mu[:])
+        for (block, first, nodes, y_piece), z in zip(reversed(short), centred):
+            nc.vector.tensor_scalar(z[:], z[:], gain[:], 0.0, ALU.mult, ALU.max)
+            nc.sync.dma_start(out[block * P : (block + 1) * P, first : first + nodes], z[:])
         for block, first, nodes, y_piece in whole:
             normed = held.tile([P, nodes], F32, name=f"normed{block}_{first}")
             nc.scalar.activation(

@@ -17,7 +17,9 @@ PIECES = (
     ((0, 512), (512, 512)),
     ((0, 512), (512, 384), (896, 128)),
 )
-N_PIECES = sum(len(cut) for cut in PIECES)
+CHUNK = 128
+TRIPLES = 2 * BLOCKS * NODES // CHUNK
+COUNT = CHUNK // 2
 
 FLOPS = 2 * TAPS * P * FEATURES * NODES
 
@@ -41,8 +43,10 @@ def tile_net_latency_kernel(tc, x, w_self, w_left, w_right, b, offs, out):
         with nc.allow_non_contiguous_dma(reason="256 floats, one to a partition and block"):
             nc.sync.dma_start(bias[:], b.rearrange("(k p) o -> p (k o)", p=P))
 
-        averager = held.tile([P, P], F32, name="averager")
-        nc.vector.memset(averager[:], 1.0 / P)
+        averager = held.tile([P, P], BF16, name="averager")
+        nc.gpsimd.memset(averager[:], 1.0 / P)
+        mean_of_sums = held.tile([P, P], F32, name="mean_of_sums")
+        nc.gpsimd.memset(mean_of_sums[:], 1.0 / (P * TRIPLES))
         n = FEATURES * NODES
         bessel = n / (n - 1.0)
         spread = held.tile([P, 2], F32, name="spread")
@@ -54,10 +58,11 @@ def tile_net_latency_kernel(tc, x, w_self, w_left, w_right, b, offs, out):
         rel_bias = held.tile([P, BLOCKS], F32, name="rel_bias")
         nc.vector.tensor_scalar(rel_bias[:], bias[:], last_bias, None, ALU.subtract)
 
-        stats = held.tile([P, N_PIECES * 6], F32, name="stats")
+        stats = held.tile([P, TRIPLES * 3], F32, name="stats")
+        triples = stats[:].rearrange("p (t c) -> p c t", c=3)
+        means = triples[:, 1, :]
         y = []
         for block, cut in enumerate(PIECES):
-            block_start = len(y) * 6
             banks = [psum.tile([P, nodes], F32, name=f"y{len(y) + i}") for i, (first, nodes) in enumerate(cut)]
             if block < BLOCKS - 1:
                 order = [(tap, i) for tap in range(TAPS) for i in range(len(cut))]
@@ -74,29 +79,46 @@ def tile_net_latency_kernel(tc, x, w_self, w_left, w_right, b, offs, out):
                     stop=(tap == TAPS - 1),
                 )
                 if tap == TAPS - 1:
-                    nc.vector.bn_stats(stats[:, len(y) * 6 : (len(y) + 1) * 6], banks[i][:])
-                    if not y:
-                        sample = held.tile([P, 1], F32, name="sample")
-                        nc.vector.tensor_scalar(sample[:], stats[:, 1:2], bias[:, block : block + 1], None, ALU.add)
                     y.append((block, first, nodes, banks[i]))
+                    for start in range(first, first + nodes, CHUNK):
+                        place = (block * NODES + start) // CHUNK * 6
+                        nc.vector.bn_stats(
+                            stats[:, place : place + 6], banks[i][:, start - first : start - first + CHUNK]
+                        )
             if block < BLOCKS - 1:
-                triples = stats[:, block_start : len(y) * 6]
-                means = triples.rearrange("p (t c) -> p t c", c=3)[:, :, 1:2]
-                nc.vector.tensor_scalar(means, means, rel_bias[:, block : block + 1], None, ALU.add)
+                bank_means = means[:, 0 : 2 * BANK // CHUNK]
+                bank_sum = held.tile([P, 1], F32, name="bank_sum")
+                nc.vector.tensor_reduce(bank_sum[:], bank_means, axis=mybir.AxisListType.X, op=ALU.add)
+                sample = held.tile([P, 1], BF16, name="sample")
+                nc.vector.tensor_scalar(
+                    sample[:], bank_sum[:], CHUNK / (2.0 * BANK), bias[:, 0:1], ALU.mult, ALU.add
+                )
+                block_means = means[:, 0 : 2 * NODES // CHUNK]
+                nc.vector.tensor_scalar(block_means, block_means, rel_bias[:, 0:1], None, ALU.add)
 
-        row = held.tile([P, 2], F32, name="row")
-        nc.vector.bn_aggr(row[:], stats[:])
         pivot = psum.tile([P, 1], F32, name="pivot")
         nc.tensor.matmul(pivot[:], averager[:], sample[:], start=True, stop=True)
-        terms = held.tile([P, BLOCKS + 1], F32, name="terms")
-        pivoted_bias, last_terms = terms[:, 0:BLOCKS], terms[:, BLOCKS - 1 : BLOCKS + 1]
-        nc.vector.tensor_scalar(pivoted_bias, bias[:], pivot[:], None, ALU.subtract)
+        pivoted_bias = held.tile([P, BLOCKS], F32, name="pivoted_bias")
+        nc.vector.tensor_scalar(pivoted_bias[:], bias[:], pivot[:], None, ALU.subtract)
+        last_pivoted_bias = pivoted_bias[:, BLOCKS - 1 : BLOCKS]
+        variances = held.tile([P, 2], F32, name="variances")
+        nc.vector.tensor_scalar(
+            variances[:, 0:1], last_bias, sample[:], float(TRIPLES), ALU.subtract, ALU.mult
+        )
+        scratch = held.tile([P, 2 * TRIPLES], F32, name="scratch")
+        nc.vector.tensor_scalar(
+            scratch[:, 0:TRIPLES], triples[:, 2, :], 1.0 / COUNT, None, ALU.mult, ALU.add,
+            accum_out=variances[:, 1:2],
+        )
+        squares = held.tile([P, 2], F32, name="squares")
+        nc.vector.tensor_reduce(squares[:, 0:1], means, axis=mybir.AxisListType.X, op=ALU.add)
         nc.scalar.activation(
-            terms[:, BLOCKS : BLOCKS + 1], row[:, 0:1], ACT.Square, bias=terms[:, BLOCKS - 1 : BLOCKS]
+            scratch[:, TRIPLES : 2 * TRIPLES], means, ACT.Square, bias=last_pivoted_bias,
+            accum_out=squares[:, 1:2],
         )
         moments = psum.tile([P, 2], F32, name="moments")
-        nc.tensor.matmul(moments[:], averager[:], row[:], start=True, stop=False)
-        nc.tensor.matmul(moments[:], averager[:], last_terms, start=False, stop=True)
+        nc.tensor.matmul(moments[:], mean_of_sums[:], variances[:], start=True, stop=False)
+        nc.tensor.matmul(moments[:], mean_of_sums[:], squares[:], start=False, stop=True)
         m, mean_square = moments[:, 0:1], moments[:, 1:2]
 
         short = [piece for piece in y if piece[2] < BANK]
@@ -104,12 +126,12 @@ def tile_net_latency_kernel(tc, x, w_self, w_left, w_right, b, offs, out):
         centred = []
         for block, first, nodes, y_piece in reversed(short):
             z = held.tile([P, nodes], F32, name=f"z{block}_{first}")
-            nc.vector.tensor_scalar(z[:], y_piece[:], terms[:, block : block + 1], None, ALU.add)
+            nc.vector.tensor_scalar(z[:], y_piece[:], last_pivoted_bias, None, ALU.add)
             centred.append(z)
 
         nc.vector.tensor_scalar(spread[:, 0:1], m, m, mean_square, ALU.mult, ALU.subtract)
         centre = held.tile([P, BLOCKS], F32, name="centre")
-        nc.vector.tensor_scalar(centre[:], pivoted_bias, m, None, ALU.subtract)
+        nc.vector.tensor_scalar(centre[:], pivoted_bias[:], m, None, ALU.subtract)
         for z in centred:
             nc.vector.tensor_scalar(z[:], z[:], m, None, ALU.subtract)
 

@@ -30,10 +30,10 @@ def tile_net_latency_kernel(tc, x, w_self, w_left, w_right, b, offs, out):
         tc.tile_pool(name="held", bufs=1) as held,
         tc.psum_pool(name="psum", bufs=1) as psum,
     ):
+        table = held.tile([P, NODES], BF16, name="table")
+        nc.sync.dma_start(table[:], x)
         offsets = held.tile([P, TAPS * NODES // 16], U16, name="offsets")
         nc.sync.dma_start(offsets[:], offs)
-        table = held.tile([P, NODES], BF16, name="table")
-        nc.scalar.dma_start(table[:], x)
         weights = []
         for tap, w in enumerate((w_self, w_left, w_right)):
             w_tile = held.tile([P, FEATURES], BF16, name=f"w{tap}")

import concourse.mybir as mybir

BF16, F32, U16 = mybir.dt.bfloat16, mybir.dt.float32, mybir.dt.uint16
ALU = mybir.AluOpType
ACT = mybir.ActivationFunctionType

P = 128
NODES = 1024
FEATURES = 256
TAPS = 3
BLOCKS = FEATURES // P
BANK = 512
EPS = 1e-5
NEVER_NEGATIVE = (1e-3 * EPS) ** 2

PIECES = (
    ((0, 512), (512, 512)),
    ((0, 512), (512, 384), (896, 128)),
)
CHUNK = 128
TRIPLES = 2 * BLOCKS * NODES // CHUNK
COUNT = CHUNK // 2

FLOPS = 2 * TAPS * P * FEATURES * NODES


def tile_net_latency_kernel(tc, x, w_self, w_left, w_right, b, offs, out):
    nc = tc.nc
    with (
        tc.tile_pool(name="held", bufs=1) as held,
        tc.psum_pool(name="psum", bufs=1) as psum,
    ):
        table = held.tile([P, NODES], BF16, name="table")
        nc.sync.dma_start(table[:], x)
        offsets = held.tile([P, TAPS * NODES // 16], U16, name="offsets")
        nc.sync.dma_start(offsets[:], offs)
        weights = []
        for tap, w in enumerate((w_self, w_left, w_right)):
            w_tile = held.tile([P, FEATURES], BF16, name=f"w{tap}")
            nc.sync.dma_start(w_tile[:], w)
            weights.append(w_tile)
        bias = held.tile([P, BLOCKS], F32, name="bias")
        with nc.allow_non_contiguous_dma(reason="256 floats, one to a partition and block"):
            nc.sync.dma_start(bias[:], b.rearrange("(k p) o -> p (k o)", p=P))

        averager = held.tile([P, P], BF16, name="averager")
        nc.gpsimd.memset(averager[:], 1.0 / P)
        mean_of_sums = held.tile([P, P], F32, name="mean_of_sums")
        nc.gpsimd.memset(mean_of_sums[:], 1.0 / (P * TRIPLES))
        n = FEATURES * NODES
        bessel = n / (n - 1.0)
        spread = held.tile([P, 2], F32, name="spread")
        nc.vector.memset(spread[:, 1:2], -EPS * EPS / bessel)
        roots = held.tile([P, 2], F32, name="roots")
        nc.scalar.activation(roots[:, 1:2], spread[:, 1:2], ACT.Sqrt, bias=NEVER_NEGATIVE, scale=-bessel)

        last_bias = bias[:, BLOCKS - 1 : BLOCKS]
        rel_bias = held.tile([P, BLOCKS], F32, name="rel_bias")
        nc.vector.tensor_scalar(rel_bias[:], bias[:], last_bias, None, ALU.subtract)

        stats = held.tile([P, TRIPLES * 3], F32, name="stats")
        triples = stats[:].rearrange("p (t c) -> p c t", c=3)
        means = triples[:, 1, :]
        y = []
        for block, cut in enumerate(PIECES):
            banks = [psum.tile([P, nodes], F32, name=f"y{len(y) + i}") for i, (first, nodes) in enumerate(cut)]
            if block < BLOCKS - 1:
                order = [(tap, i) for tap in range(TAPS) for i in range(len(cut))]
            else:
                order = [(tap, i) for i in range(len(cut)) for tap in range(TAPS)]
            for tap, i in order:
                first, nodes = cut[i]
                column = (tap * NODES + first) // 16
                nc.tensor.matmul(
                    banks[i][:],
                    weights[tap][:, block * P : (block + 1) * P],
                    table[:].indirect(offsets[:, column : column + nodes // 16]),
                    start=(tap == 0),
                    stop=(tap == TAPS - 1),
                )
                if tap == TAPS - 1:
                    y.append((block, first, nodes, banks[i]))
                    for start in range(first, first + nodes, CHUNK):
                        place = (block * NODES + start) // CHUNK * 6
                        nc.vector.bn_stats(
                            stats[:, place : place + 6], banks[i][:, start - first : start - first + CHUNK]
                        )
            if block < BLOCKS - 1:
                bank_means = means[:, 0 : 2 * BANK // CHUNK]
                bank_sum = held.tile([P, 1], F32, name="bank_sum")
                nc.vector.tensor_reduce(bank_sum[:], bank_means, axis=mybir.AxisListType.X, op=ALU.add)
                sample = held.tile([P, 1], BF16, name="sample")
                nc.vector.tensor_scalar(
                    sample[:], bank_sum[:], CHUNK / (2.0 * BANK), bias[:, 0:1], ALU.mult, ALU.add
                )
                block_means = means[:, 0 : 2 * NODES // CHUNK]
                nc.vector.tensor_scalar(block_means, block_means, rel_bias[:, 0:1], None, ALU.add)

        pivot = psum.tile([P, 1], F32, name="pivot")
        nc.tensor.matmul(pivot[:], averager[:], sample[:], start=True, stop=True)
        pivoted_bias = held.tile([P, BLOCKS], F32, name="pivoted_bias")
        nc.vector.tensor_scalar(pivoted_bias[:], bias[:], pivot[:], None, ALU.subtract)
        last_pivoted_bias = pivoted_bias[:, BLOCKS - 1 : BLOCKS]
        variances = held.tile([P, 2], F32, name="variances")
        nc.vector.tensor_scalar(
            variances[:, 0:1], last_bias, sample[:], float(TRIPLES), ALU.subtract, ALU.mult
        )
        scratch = held.tile([P, 2 * TRIPLES], F32, name="scratch")
        nc.vector.tensor_scalar(
            scratch[:, 0:TRIPLES], triples[:, 2, :], 1.0 / COUNT, None, ALU.mult, ALU.add,
            accum_out=variances[:, 1:2],
        )
        squares = held.tile([P, 2], F32, name="squares")
        nc.vector.tensor_reduce(squares[:, 0:1], means, axis=mybir.AxisListType.X, op=ALU.add)
        nc.scalar.activation(
            scratch[:, TRIPLES : 2 * TRIPLES], means, ACT.Square, bias=last_pivoted_bias,
            accum_out=squares[:, 1:2],
        )
        moments = psum.tile([P, 2], F32, name="moments")
        nc.tensor.matmul(moments[:], mean_of_sums[:], variances[:], start=True, stop=False)
        nc.tensor.matmul(moments[:], mean_of_sums[:], squares[:], start=False, stop=True)
        m, mean_square = moments[:, 0:1], moments[:, 1:2]

        short = [piece for piece in y if piece[2] < BANK]
        whole = [piece for piece in y if piece[2] == BANK]
        centred = []
        for block, first, nodes, y_piece in reversed(short):
            z = held.tile([P, nodes], F32, name=f"z{block}_{first}")
            nc.vector.tensor_scalar(z[:], y_piece[:], last_pivoted_bias, None, ALU.add)
            centred.append(z)

        nc.vector.tensor_scalar(spread[:, 0:1], m, m, mean_square, ALU.mult, ALU.subtract)
        centre = held.tile([P, BLOCKS], F32, name="centre")
        nc.vector.tensor_scalar(centre[:], pivoted_bias[:], m, None, ALU.subtract)
        for z in centred:
            nc.vector.tensor_scalar(z[:], z[:], m, None, ALU.subtract)

        sd_eps = held.tile([P, 1], F32, name="sd_eps")
        nc.scalar.activation(
            roots[:], spread[:], ACT.Sqrt, bias=NEVER_NEGATIVE, scale=-bessel, accum_out=sd_eps[:]
        )
        gain = held.tile([P, 1], F32, name="gain")
        nc.vector.reciprocal(gain[:], sd_eps[:])
        shift = held.tile([P, BLOCKS], F32, name="shift")
        nc.scalar.activation(shift[:], centre[:], ACT.Identity, scale=gain[:])

        for (block, first, nodes, y_piece), z in zip(reversed(short), centred):
            nc.vector.tensor_scalar(z[:], z[:], gain[:], 0.0, ALU.mult, ALU.max)
            nc.sync.dma_start(out[block * P : (block + 1) * P, first : first + nodes], z[:])
        for block, first, nodes, y_piece in whole:
            normed = held.tile([P, nodes], F32, name=f"normed{block}_{first}")
            nc.scalar.activation(
                normed[:], y_piece[:], ACT.Relu, bias=shift[:, block : block + 1], scale=gain[:]
            )
            nc.sync.dma_start(out[block * P : (block + 1) * P, first : first + nodes], normed[:])
